import numpy as np
import ml_dtypes


def mxq(x, axis, fmt="e4m3"):
    dtype, down = {"e4m3": (ml_dtypes.float8_e4m3fn, 7), "e5m2": (ml_dtypes.float8_e5m2, 14)}[fmt]
    v = np.moveaxis(np.asarray(x, np.float32).astype(ml_dtypes.bfloat16).astype(np.float64), axis, -1)
    blocks = v.reshape(v.shape[:-1] + (-1, 32))
    amax = np.abs(blocks).max(-1, keepdims=True)
    byte = np.maximum(np.where(amax > 0, np.frexp(amax)[1] - 1 + 127, 0) - down, 1)
    scale = np.exp2(byte - 127.0)
    codes = (blocks / scale).astype(np.float32).astype(dtype).astype(np.float64)
    return np.moveaxis((codes * scale).reshape(v.shape), -1, axis)


WIDE = False


def mx_kscale(k):
    if not WIDE:
        return np.ones(k)
    levels = np.array([10, -10, 5, -5, 0])
    a = np.random.permutation(np.resize(levels, k // 512 * 4)).reshape(k // 512, 4)
    idx = np.arange(k)
    return np.exp2(a[idx // 512, idx % 128 // 32])


BF16 = ml_dtypes.bfloat16


def bf(x):
    return np.asarray(x, np.float32).astype(BF16)


def f64(x):
    return np.asarray(x).astype(np.float64)


E2M1 = np.array([0.0, 0.5, 1.0, 1.5, 2.0, 3.0, 4.0, 6.0, -0.0, -0.5, -1.0, -1.5, -2.0, -3.0, -4.0, -6.0])


def pack_weight(w, fmt):
    k, n = w.shape
    w = f64(bf(w)).reshape(k // 32, 32, n)
    amax = np.abs(w).max(1)
    if fmt == "e4m3":
        byte = np.frexp(amax)[1] - 1 + 127 - 7
    else:
        mant, ex = np.frexp(amax / 6.0)
        byte = np.where(mant > 0.5, ex, ex - 1) + 127
    byte = np.clip(np.where(amax > 0, byte, 1), 1, 254)
    scaled = (w * np.exp2(127.0 - byte)[:, None, :]).reshape(k, n).astype(np.float32)
    by_word = np.ascontiguousarray(scaled.reshape(k // 512, 128, 4, n).transpose(0, 1, 3, 2))
    if fmt == "e4m3":
        words = by_word.astype(ml_dtypes.float8_e4m3fn).view(np.uint8)
    else:
        c = by_word.astype(ml_dtypes.float4_e2m1fn).view(np.uint8) & 0xF
        words = c[..., 0::2] | (c[..., 1::2] << 4)
    return np.ascontiguousarray(words), np.ascontiguousarray(byte.astype(np.uint8).reshape(k // 512, 16, n))


def unpack_weight(words, scales, fmt):
    g, p, n, _ = words.shape
    if fmt == "e4m3":
        vals = np.ascontiguousarray(words).view(ml_dtypes.float8_e4m3fn).astype(np.float64)
    else:
        nib = np.empty((g, p, n, 4), np.uint8)
        nib[..., 0::2] = words & 0xF
        nib[..., 1::2] = words >> 4
        vals = E2M1[nib]
    vals = vals * np.repeat(np.exp2(scales.astype(np.float64) - 127.0), 8, axis=1)[..., None]
    return vals.transpose(0, 1, 3, 2).reshape(g * 512, n)

def pack4(w):
    words, scales = pack_weight(w, "e2m1")
    return words.reshape(words.shape[0], 128, -1), scales


def unpack4(words, scales):
    return unpack_weight(words.reshape(words.shape[0], 128, -1, 2), scales, "e2m1")


B, IN, OUT, R, Q, ORD = 16384, 1024, 1024, 8, 256, 3
K = R ** ORD


def setup_inputs():
    s = mx_kscale(K)[np.arange(R) * (K // R + R)]
    z = np.random.standard_normal((ORD, R, B))
    z[ORD - 1] *= s[:, None]
    g = np.random.standard_normal((Q, K)) / np.sqrt(K) / np.repeat(s, K // R)
    words, scales = pack4(np.ascontiguousarray(g.T))
    return {"z": bf(z), "G2_words": words, "G2_scales": scales}


def reference(z, G2_words, G2_scales):
    Z = f64(z)
    kron = Z[0]
    for j in range(1, ORD):
        kron = kron[None] * Z[j].reshape((R,) + (1,) * j + (B,))
    kron = kron.reshape((-1, B))
    return unpack4(G2_words, G2_scales).T @ mxq(kron, 0, "e4m3")

@@ -1,0 +1,185 @@
+from contextlib import ExitStack
+
+import concourse.mybir as mybir
+from concourse.masks import make_identity
+
+F32 = mybir.dt.float32
+BF16 = mybir.dt.bfloat16
+I32 = mybir.dt.int32
+U32 = mybir.dt.uint32
+U8 = mybir.dt.uint8
+FP8X4 = mybir.dt.float8_e4m3fn_x4
+FP4X4 = mybir.dt.float4_e2m1fn_x4
+MULT = mybir.AluOpType.mult
+COPY = mybir.ActivationFunctionType.Copy
+
+P = 128
+RANK = 8
+SAMPLES = 16384
+CHUNKS = 16
+CHUNK = SAMPLES // CHUNKS
+TILES = CHUNK // P
+BLOCK = 512
+BLOCK_TILES = BLOCK // P
+BLOCKS = SAMPLES // BLOCK
+SCALAR_C = 1
+
+FLOPS = 2 * 256 * 512 * SAMPLES
+
+
+def tile_fast_tucker_taylor_pa_t_kernel(tc, z, G2_words, G2_scales, out):
+    nc = tc.nc
+    with ExitStack() as ctx:
+        const = ctx.enter_context(tc.tile_pool(name="const", bufs=1))
+
+        zk = const.tile([P, 3, CHUNK], BF16)
+        for u in range(2):
+            for h in range(2):
+                first = 64 * u + 32 * h
+                row = 4 * h + 2 * u
+                nc.sync.dma_start(
+                    out=zk[first : first + 32, 0, :],
+                    in_=z[0, row : row + 2, :].rearrange("e (ch m) -> (e ch) m", ch=CHUNKS),
+                )
+        for j in (1, 2):
+            nc.sync.dma_start(
+                out=zk[:, j, :], in_=z[j].rearrange("r (ch m) -> (r ch) m", ch=CHUNKS)
+            )
+        g2_words = const.tile([P, 512], U8, align_bytes=64)
+        nc.sync.dma_start(out=g2_words[:].bitcast(I32), in_=G2_words[0].bitcast(I32))
+        g2_scales = const.tile([P, 256], U8, align_bytes=64)
+        nc.vector.memset(g2_scales[:].bitcast(I32), 0)
+        for quad in range(4):
+            nc.sync.dma_start(
+                out=g2_scales[32 * quad : 32 * quad + 4, :].bitcast(I32),
+                in_=G2_scales[0, 4 * quad : 4 * quad + 4, :].bitcast(I32),
+            )
+
+        ident_bf16 = const.tile([P, P], BF16)
+        make_identity(nc, ident_bf16[:])
+        ident_f32 = const.tile([P, P], F32)
+        make_identity(nc, ident_f32[:])
+
+        zT = const.tile([P, 3, TILES, RANK, CHUNKS], F32)
+        with tc.psum_pool(name="zt_psum", bufs=1) as zt_psum:
+            for j in range(3):
+                zt = zt_psum.tile([P, TILES, P], BF16, name="zt%d" % j)
+                for i in range(TILES):
+                    nc.tensor.transpose(zt[:, i, :], zk[:, j, P * i : P * (i + 1)], ident_bf16[:])
+                copy_out = nc.scalar.copy if j == 1 else nc.vector.tensor_copy
+                copy_out(
+                    out=zT[:, j].rearrange("p i r ch -> p (i r ch)"),
+                    in_=zt[:].rearrange("p i x -> p (i x)"),
+                )
+
+        pair_pool = ctx.enter_context(tc.tile_pool(name="pair", bufs=2))
+        kron_pool = ctx.enter_context(tc.tile_pool(name="kron", bufs=3))
+        group_pool = ctx.enter_context(tc.tile_pool(name="group", bufs=3))
+        mx_pool = ctx.enter_context(tc.tile_pool(name="mx", bufs=3))
+        res_pool = ctx.enter_context(tc.tile_pool(name="res", bufs=3))
+        xt_psum = ctx.enter_context(tc.psum_pool(name="xt_psum", bufs=4))
+        acc_psum = ctx.enter_context(tc.psum_pool(name="acc_psum", bufs=4))
+
+        out_view = out.rearrange("(hq q) n -> q hq n", hq=2)
+        kron_tiles = {}
+        turned_tiles = {}
+        grouped_tiles = {}
+        mx_tiles = {}
+        acc_tiles = {}
+
+        def build(t):
+            ch = t // 2
+            tile0 = BLOCK_TILES * (t % 2)
+            tiles = slice(tile0, tile0 + BLOCK_TILES)
+            w01 = pair_pool.tile([P, BLOCK_TILES, 2, RANK, 4], F32, name="w01")
+            for u in range(2):
+                nc.vector.tensor_tensor(
+                    out=w01[:, :, u, :, :],
+                    in0=zT[:, 0, tiles, 4 * u : 4 * u + 4, ch]
+                    .unsqueeze(2)
+                    .to_broadcast([P, BLOCK_TILES, RANK, 4]),
+                    in1=zT[:, 1, tiles, :, ch].unsqueeze(3).to_broadcast([P, BLOCK_TILES, RANK, 4]),
+                    op=MULT,
+                )
+            kronT = kron_pool.tile([P, BLOCK_TILES, 2, RANK, 32], BF16, name="kronT")
+            kron_tiles[t] = kronT
+            for ii in range(BLOCK_TILES):
+                pair = w01[:, ii].rearrange("p u b x -> p u (b x)")
+                for c in range(RANK):
+                    z2 = zT[:, 2, tile0 + ii, c, ch : ch + 1]
+                    if c < RANK - SCALAR_C:
+                        nc.vector.tensor_scalar(
+                            out=kronT[:, ii, :, c, :], in0=pair, scalar1=z2, scalar2=None, op0=MULT
+                        )
+                    else:
+                        nc.scalar.activation(out=kronT[:, ii, :, c, :], in_=pair, func=COPY, scale=z2)
+
+        def turn(t):
+            kronT = kron_tiles.pop(t)
+            turned_tiles[t] = []
+            for bank in range(2):
+                xt = xt_psum.tile([P, 2, 2, P], F32, name="xt")
+                turned_tiles[t].append(xt)
+                for i2 in range(2):
+                    for u in range(2):
+                        nc.tensor.transpose(
+                            xt[:, i2, u, :],
+                            kronT[:, 2 * bank + i2, u].rearrange("p c x -> p (c x)").bitcast(F32),
+                            ident_f32[:],
+                        )
+
+        def regroup(t):
+            grouped = group_pool.tile([P, 4 * BLOCK], BF16, align_bytes=64, name="grouped")
+            grouped_tiles[t] = grouped
+            grouped_words = grouped[:].bitcast(F32).rearrange(
+                "p (ii n u) -> p ii n u", ii=BLOCK_TILES, u=2
+            )
+            for bank, xt in enumerate(turned_tiles.pop(t)):
+                nc.scalar.copy(
+                    out=grouped_words[:, 2 * bank : 2 * bank + 2],
+                    in_=xt[:].rearrange("p s u n -> p s n u"),
+                )
+
+        def quantise(t):
+            grouped = grouped_tiles.pop(t)
+            codes = mx_pool.tile([P, BLOCK], U32, align_bytes=64, name="codes")
+            scales = mx_pool.tile([P, BLOCK], U8, align_bytes=64, name="scales")
+            mx_tiles[t] = (codes, scales)
+            nc.vector.quantize_mx(out=codes[:].bitcast(FP8X4), scales=scales[:], in_=grouped[:])
+
+        def multiply(t):
+            codes, scales = mx_tiles.pop(t)
+            acc_tiles[t] = []
+            for hq in range(2):
+                acc = acc_psum.tile([P, BLOCK], F32, name="acc")
+                acc_tiles[t].append(acc)
+                nc.tensor.matmul_mx(
+                    out=acc[:],
+                    lhsT=g2_words[:, 256 * hq : 256 * (hq + 1)].bitcast(FP4X4),
+                    lhsT_scale=g2_scales[:, P * hq : P * (hq + 1)],
+                    rhs=codes[:].bitcast(FP8X4),
+                    rhs_scale=scales[:],
+                    start=True,
+                    stop=True,
+                )
+
+        def store(t):
+            res = res_pool.tile([P, 2, BLOCK], F32, name="res")
+            for hq, acc in enumerate(acc_tiles.pop(t)):
+                nc.scalar.copy(out=res[:, hq, :], in_=acc[:])
+            nc.sync.dma_start(out=out_view[:, :, BLOCK * t : BLOCK * (t + 1)], in_=res[:])
+
+        with tc.manual_schedule():
+            for step in range(BLOCKS + 4):
+                if 0 <= step - 3 < BLOCKS:
+                    quantise(step - 3)
+                if 0 <= step - 1 < BLOCKS:
+                    turn(step - 1)
+                if 0 <= step - 3 < BLOCKS:
+                    multiply(step - 3)
+                if 0 <= step - 2 < BLOCKS:
+                    regroup(step - 2)
+                if 0 <= step - 4 < BLOCKS:
+                    store(step - 4)
+                if step < BLOCKS:
+                    build(step)

@@ -16,13 +16,14 @@ COPY = mybir.ActivationFunctionType.Copy
 P = 128
 RANK = 8
 SAMPLES = 16384
-CHUNKS = 16
-CHUNK = SAMPLES // CHUNKS
-TILES = CHUNK // P
 BLOCK = 512
 BLOCK_TILES = BLOCK // P
 BLOCKS = SAMPLES // BLOCK
-SCALAR_C = 1
+ROUND_BLOCKS = 4
+VECTOR_BLOCKS = 3
+ROUND = ROUND_BLOCKS * BLOCK
+ROUND_TILES = ROUND // P
+ROUNDS = SAMPLES // ROUND
 
 FLOPS = 2 * 256 * 512 * SAMPLES
 
@@ -31,113 +32,186 @@ def tile_fast_tucker_taylor_pa_t_kernel(tc, z, G2_words, G2_scales, out):
     nc = tc.nc
     with ExitStack() as ctx:
         const = ctx.enter_context(tc.tile_pool(name="const", bufs=1))
-
-        zk = const.tile([P, 3, CHUNK], BF16)
-        for u in range(2):
-            for h in range(2):
-                first = 64 * u + 32 * h
-                row = 4 * h + 2 * u
-                nc.sync.dma_start(
-                    out=zk[first : first + 32, 0, :],
-                    in_=z[0, row : row + 2, :].rearrange("e (ch m) -> (e ch) m", ch=CHUNKS),
-                )
-        for j in (1, 2):
-            nc.sync.dma_start(
-                out=zk[:, j, :], in_=z[j].rearrange("r (ch m) -> (r ch) m", ch=CHUNKS)
-            )
-        g2_words = const.tile([P, 512], U8, align_bytes=64)
-        nc.sync.dma_start(out=g2_words[:].bitcast(I32), in_=G2_words[0].bitcast(I32))
-        g2_scales = const.tile([P, 256], U8, align_bytes=64)
-        nc.vector.memset(g2_scales[:].bitcast(I32), 0)
-        for quad in range(4):
-            nc.sync.dma_start(
-                out=g2_scales[32 * quad : 32 * quad + 4, :].bitcast(I32),
-                in_=G2_scales[0, 4 * quad : 4 * quad + 4, :].bitcast(I32),
-            )
-
-        ident_bf16 = const.tile([P, P], BF16)
-        make_identity(nc, ident_bf16[:])
-        ident_f32 = const.tile([P, P], F32)
-        make_identity(nc, ident_f32[:])
-
-        zT = const.tile([P, 3, TILES, RANK, CHUNKS], F32)
-        with tc.psum_pool(name="zt_psum", bufs=1) as zt_psum:
-            for j in range(3):
-                zt = zt_psum.tile([P, TILES, P], BF16, name="zt%d" % j)
-                for i in range(TILES):
-                    nc.tensor.transpose(zt[:, i, :], zk[:, j, P * i : P * (i + 1)], ident_bf16[:])
-                copy_out = nc.scalar.copy if j == 1 else nc.vector.tensor_copy
-                copy_out(
-                    out=zT[:, j].rearrange("p i r ch -> p (i r ch)"),
-                    in_=zt[:].rearrange("p i x -> p (i x)"),
-                )
-
-        pair_pool = ctx.enter_context(tc.tile_pool(name="pair", bufs=2))
-        kron_pool = ctx.enter_context(tc.tile_pool(name="kron", bufs=3))
+        zk_pool = ctx.enter_context(tc.tile_pool(name="zk", bufs=3))
+        z0g_pool = ctx.enter_context(tc.tile_pool(name="z0g", bufs=3))
+        factor_pool = ctx.enter_context(tc.tile_pool(name="factor", bufs=2))
+        pair_pool = ctx.enter_context(tc.tile_pool(name="pair", bufs=3))
+        kron_pool = ctx.enter_context(tc.tile_pool(name="kron", bufs=2))
         group_pool = ctx.enter_context(tc.tile_pool(name="group", bufs=3))
         mx_pool = ctx.enter_context(tc.tile_pool(name="mx", bufs=3))
-        res_pool = ctx.enter_context(tc.tile_pool(name="res", bufs=3))
-        xt_psum = ctx.enter_context(tc.psum_pool(name="xt_psum", bufs=4))
+        res_pool = ctx.enter_context(tc.tile_pool(name="res", bufs=6))
+        zt_psum = ctx.enter_context(tc.psum_pool(name="zt_psum", bufs=1))
+        turned_psum = ctx.enter_context(tc.psum_pool(name="turned_psum", bufs=3))
         acc_psum = ctx.enter_context(tc.psum_pool(name="acc_psum", bufs=4))
 
         out_view = out.rearrange("(hq q) n -> q hq n", hq=2)
+        zk_tiles = {}
+        z0g_tiles = {}
+        zt_tiles = {}
+        factor_tiles = {}
+        pair_tiles = {}
         kron_tiles = {}
         turned_tiles = {}
         grouped_tiles = {}
         mx_tiles = {}
         acc_tiles = {}
 
-        def build(t):
-            ch = t // 2
-            tile0 = BLOCK_TILES * (t % 2)
+        def is_block(t):
+            return 0 <= t < BLOCKS
+
+        def is_scalar_block(t):
+            return t % ROUND_BLOCKS >= VECTOR_BLOCKS
+
+        def load_round(r):
+            samples = slice(ROUND * r, ROUND * (r + 1))
+            zk = zk_pool.tile([P, 3, P], BF16, name="zk")
+            zk_tiles[r] = zk
+            for j in (2, 1, 0):
+                nc.sync.dma_start(
+                    out=zk[:, j, :],
+                    in_=z[j, :, samples].rearrange("r (ch m) -> r ch m", ch=ROUND_TILES),
+                )
+            width = VECTOR_BLOCKS * BLOCK
+            z0g = z0g_pool.tile([P, 4, width], BF16, name="z0g")
+            z0g_tiles[r] = z0g
+            piece = BLOCK if r == 0 else width
+            for first in range(0, width, piece):
+                for h in range(2):
+                    nc.sync.dma_start(
+                        out=z0g[h:P:2, :, first : first + piece],
+                        in_=z[0, 4 * h : 4 * h + 4, ROUND * r + first : ROUND * r + first + piece]
+                        .unsqueeze(0)
+                        .to_broadcast([P // 2, 4, piece]),
+                    )
+
+        def turn_factors(r):
+            zk = zk_tiles.pop(r)
+            zt = zt_psum.tile([P, 3, P], BF16, name="zt")
+            zt_tiles[r] = zt
+            for j in (2, 1, 0):
+                nc.tensor.transpose(zt[:, j, :], zk[:, j, :], ident_bf16[:])
+
+        def copy_factors(r):
+            zt = zt_tiles.pop(r)
+            z2T = factor_pool.tile([P, RANK, ROUND_TILES], F32, name="z2T")
+            z1T = factor_pool.tile([P, RANK, 2, ROUND_TILES], F32, name="z1T")
+            z0T = factor_pool.tile([P, RANK, ROUND_TILES], F32, name="z0T")
+            factor_tiles[r] = (z0T, z1T, z2T)
+            nc.scalar.copy(out=z2T[:].rearrange("p c ch -> p (c ch)"), in_=zt[:, 2, :])
+            nc.scalar.copy(
+                out=z1T[:],
+                in_=zt[:, 1, :]
+                .rearrange("p (b ch) -> p b ch", b=RANK)
+                .unsqueeze(2)
+                .to_broadcast([P, RANK, 2, ROUND_TILES]),
+            )
+            nc.scalar.copy(
+                out=z0T[:].rearrange("p (u h e) ch -> p u h (e ch)", u=2, h=2),
+                in_=zt[:, 0, :].rearrange("p (h u x) -> p u h x", h=2, u=2),
+            )
+
+        def pair_products(t):
+            z0T, z1T, z2T = factor_tiles[t // ROUND_BLOCKS]
+            tile0 = BLOCK_TILES * (t % ROUND_BLOCKS)
             tiles = slice(tile0, tile0 + BLOCK_TILES)
-            w01 = pair_pool.tile([P, BLOCK_TILES, 2, RANK, 4], F32, name="w01")
-            for u in range(2):
-                nc.vector.tensor_tensor(
-                    out=w01[:, :, u, :, :],
-                    in0=zT[:, 0, tiles, 4 * u : 4 * u + 4, ch]
+            if is_scalar_block(t):
+                w01 = pair_pool.tile([P, BLOCK_TILES, 2, RANK, 4], F32, name="w01")
+                pair_tiles[t] = w01
+                for u in range(2):
+                    nc.gpsimd.tensor_tensor(
+                        out=w01[:, :, u, :, :],
+                        in0=z0T[:, 4 * u : 4 * u + 4, tiles]
+                        .rearrange("p x i -> p i x")
+                        .unsqueeze(2)
+                        .to_broadcast([P, BLOCK_TILES, RANK, 4]),
+                        in1=z1T[:, :, 0, tiles]
+                        .rearrange("p b i -> p i b")
+                        .unsqueeze(3)
+                        .to_broadcast([P, BLOCK_TILES, RANK, 4]),
+                        op=MULT,
+                    )
+            else:
+                w12 = pair_pool.tile([P, BLOCK_TILES, RANK, 2 * RANK], F32, name="w12")
+                pair_tiles[t] = w12
+                nc.gpsimd.tensor_tensor(
+                    out=w12[:],
+                    in0=z2T[:, :, tiles]
+                    .rearrange("p c i -> p i c")
+                    .unsqueeze(3)
+                    .to_broadcast([P, BLOCK_TILES, RANK, 2 * RANK]),
+                    in1=z1T[:, :, :, tiles]
+                    .rearrange("p b h i -> p i (b h)")
                     .unsqueeze(2)
-                    .to_broadcast([P, BLOCK_TILES, RANK, 4]),
-                    in1=zT[:, 1, tiles, :, ch].unsqueeze(3).to_broadcast([P, BLOCK_TILES, RANK, 4]),
+                    .to_broadcast([P, BLOCK_TILES, RANK, 2 * RANK]),
                     op=MULT,
                 )
-            kronT = kron_pool.tile([P, BLOCK_TILES, 2, RANK, 32], BF16, name="kronT")
-            kron_tiles[t] = kronT
-            for ii in range(BLOCK_TILES):
-                pair = w01[:, ii].rearrange("p u b x -> p u (b x)")
-                for c in range(RANK):
-                    z2 = zT[:, 2, tile0 + ii, c, ch : ch + 1]
-                    if c < RANK - SCALAR_C:
-                        nc.vector.tensor_scalar(
-                            out=kronT[:, ii, :, c, :], in0=pair, scalar1=z2, scalar2=None, op0=MULT
-                        )
-                    else:
-                        nc.scalar.activation(out=kronT[:, ii, :, c, :], in_=pair, func=COPY, scale=z2)
+
+        def scalar_tile(t, ii):
+            z2T = factor_tiles[t // ROUND_BLOCKS][2]
+            if ii == 0:
+                kron_tiles[t] = kron_pool.tile([P, BLOCK_TILES, 2, RANK, 32], BF16, name="kronT")
+            kronT = kron_tiles[t]
+            tile_in_round = BLOCK_TILES * (t % ROUND_BLOCKS) + ii
+            pair = pair_tiles[t][:, ii].rearrange("p u b x -> p u (b x)")
+            for c in range(RANK):
+                nc.scalar.activation(
+                    out=kronT[:, ii, :, c, :],
+                    in_=pair,
+                    func=COPY,
+                    scale=z2T[:, c, tile_in_round : tile_in_round + 1],
+                )
 
         def turn(t):
-            kronT = kron_tiles.pop(t)
             turned_tiles[t] = []
-            for bank in range(2):
-                xt = xt_psum.tile([P, 2, 2, P], F32, name="xt")
-                turned_tiles[t].append(xt)
-                for i2 in range(2):
-                    for u in range(2):
-                        nc.tensor.transpose(
-                            xt[:, i2, u, :],
-                            kronT[:, 2 * bank + i2, u].rearrange("p c x -> p (c x)").bitcast(F32),
-                            ident_f32[:],
-                        )
+            if is_scalar_block(t):
+                kronT = kron_tiles.pop(t)
+                pair_tiles.pop(t)
+                for bank in range(2):
+                    xt = turned_psum.tile([P, 2, 2, P], F32, name="turned")
+                    turned_tiles[t].append(xt)
+                    for i2 in range(2):
+                        for u in range(2):
+                            nc.tensor.transpose(
+                                xt[:, i2, u, :],
+                                kronT[:, 2 * bank + i2, u].rearrange("p c x -> p (c x)").bitcast(F32),
+                                ident_f32[:],
+                            )
+            else:
+                w12 = pair_tiles.pop(t)
+                w12_k = turned_psum.tile([P, BLOCK_TILES, P], F32, name="turned")
+                turned_tiles[t].append(w12_k)
+                for ii in range(BLOCK_TILES):
+                    nc.tensor.transpose(
+                        w12_k[:, ii, :], w12[:, ii].rearrange("p c x -> p (c x)"), ident_f32[:]
+                    )
 
-        def regroup(t):
-            grouped = group_pool.tile([P, 4 * BLOCK], BF16, align_bytes=64, name="grouped")
+        def group(t):
+            grouped = group_pool.tile([P, BLOCK, 4], BF16, align_bytes=64, name="grouped")
             grouped_tiles[t] = grouped
-            grouped_words = grouped[:].bitcast(F32).rearrange(
-                "p (ii n u) -> p ii n u", ii=BLOCK_TILES, u=2
-            )
-            for bank, xt in enumerate(turned_tiles.pop(t)):
-                nc.scalar.copy(
-                    out=grouped_words[:, 2 * bank : 2 * bank + 2],
-                    in_=xt[:].rearrange("p s u n -> p s n u"),
+            turned = turned_tiles.pop(t)
+            if is_scalar_block(t):
+                grouped_words = (
+                    grouped[:]
+                    .rearrange("p n t -> p (n t)")
+                    .bitcast(F32)
+                    .rearrange("p (ii n u) -> p ii n u", ii=BLOCK_TILES, u=2)
+                )
+                for bank, xt in enumerate(turned):
+                    nc.scalar.copy(
+                        out=grouped_words[:, 2 * bank : 2 * bank + 2],
+                        in_=xt[:].rearrange("p s u n -> p s n u"),
+                    )
+            else:
+                first = BLOCK * (t % ROUND_BLOCKS)
+                z0g = z0g_tiles[t // ROUND_BLOCKS]
+                nc.vector.tensor_tensor(
+                    out=grouped[:],
+                    in0=z0g[:, :, first : first + BLOCK].rearrange("p t n -> p n t"),
+                    in1=turned[0][:]
+                    .rearrange("p i n -> p (i n)")
+                    .unsqueeze(2)
+                    .to_broadcast([P, BLOCK, 4]),
+                    op=MULT,
                 )
 
         def quantise(t):
@@ -145,7 +219,11 @@ def tile_fast_tucker_taylor_pa_t_kernel(tc, z, G2_words, G2_scales, out):
             codes = mx_pool.tile([P, BLOCK], U32, align_bytes=64, name="codes")
             scales = mx_pool.tile([P, BLOCK], U8, align_bytes=64, name="scales")
             mx_tiles[t] = (codes, scales)
-            nc.vector.quantize_mx(out=codes[:].bitcast(FP8X4), scales=scales[:], in_=grouped[:])
+            nc.vector.quantize_mx(
+                out=codes[:].bitcast(FP8X4),
+                scales=scales[:],
+                in_=grouped[:].rearrange("p n t -> p (n t)"),
+            )
 
         def multiply(t):
             codes, scales = mx_tiles.pop(t)
@@ -164,22 +242,49 @@ def tile_fast_tucker_taylor_pa_t_kernel(tc, z, G2_words, G2_scales, out):
                 )
 
         def store(t):
-            res = res_pool.tile([P, 2, BLOCK], F32, name="res")
             for hq, acc in enumerate(acc_tiles.pop(t)):
-                nc.scalar.copy(out=res[:, hq, :], in_=acc[:])
-            nc.sync.dma_start(out=out_view[:, :, BLOCK * t : BLOCK * (t + 1)], in_=res[:])
+                res = res_pool.tile([P, BLOCK], F32, name="res")
+                nc.scalar.copy(out=res[:], in_=acc[:])
+                nc.sync.dma_start(out=out_view[:, hq, BLOCK * t : BLOCK * (t + 1)], in_=res[:])
 
         with tc.manual_schedule():
-            for step in range(BLOCKS + 4):
-                if 0 <= step - 3 < BLOCKS:
+            load_round(0)
+            ident_bf16 = const.tile([P, P], BF16)
+            make_identity(nc, ident_bf16[:])
+            ident_f32 = const.tile([P, P], F32)
+            make_identity(nc, ident_f32[:])
+            g2_words = const.tile([P, 512], U8, align_bytes=64)
+            nc.sync.dma_start(out=g2_words[:].bitcast(I32), in_=G2_words[0].bitcast(I32))
+            g2_scales = const.tile([P, 256], U8, align_bytes=64)
+            nc.vector.memset(g2_scales[:].bitcast(I32), 0)
+            for quad in range(4):
+                nc.sync.dma_start(
+                    out=g2_scales[32 * quad : 32 * quad + 4, :].bitcast(I32),
+                    in_=G2_scales[0, 4 * quad : 4 * quad + 4, :].bitcast(I32),
+                )
+
+            for step in range(-3, BLOCKS + 5):
+                if is_block(step - 2):
+                    group(step - 2)
+                if is_block(step - 3):
                     quantise(step - 3)
-                if 0 <= step - 1 < BLOCKS:
+                if is_block(step + 3) and (step + 3) % ROUND_BLOCKS == 0:
+                    turn_factors((step + 3) // ROUND_BLOCKS)
+                if is_block(step - 1):
                     turn(step - 1)
-                if 0 <= step - 3 < BLOCKS:
+                if is_block(step - 3):
                     multiply(step - 3)
-                if 0 <= step - 2 < BLOCKS:
-                    regroup(step - 2)
-                if 0 <= step - 4 < BLOCKS:
+                if is_block(step + 2) and (step + 2) % ROUND_BLOCKS == 0:
+                    copy_factors((step + 2) // ROUND_BLOCKS)
+                if is_block(step - 4):
                     store(step - 4)
-                if step < BLOCKS:
-                    build(step)
+                if is_block(step):
+                    in_round = step % ROUND_BLOCKS
+                    scalar_block = step - in_round + VECTOR_BLOCKS
+                    if not is_scalar_block(step):
+                        pair_products(step)
+                    if in_round == 0:
+                        pair_products(scalar_block)
+                    scalar_tile(scalar_block, in_round)
+                if is_block(step + 6) and (step + 6) % ROUND_BLOCKS == 0 and step + 6 > 0:
+                    load_round((step + 6) // ROUND_BLOCKS)

@@ -20,10 +20,9 @@ BLOCK = 512
 BLOCK_TILES = BLOCK // P
 BLOCKS = SAMPLES // BLOCK
 ROUND_BLOCKS = 4
-VECTOR_BLOCKS = 3
 ROUND = ROUND_BLOCKS * BLOCK
 ROUND_TILES = ROUND // P
-ROUNDS = SAMPLES // ROUND
+SCALAR_C = 0
 
 FLOPS = 2 * 256 * 512 * SAMPLES
 
@@ -33,20 +32,18 @@ def tile_fast_tucker_taylor_pa_t_kernel(tc, z, G2_words, G2_scales, out):
     with ExitStack() as ctx:
         const = ctx.enter_context(tc.tile_pool(name="const", bufs=1))
         zk_pool = ctx.enter_context(tc.tile_pool(name="zk", bufs=3))
-        z0g_pool = ctx.enter_context(tc.tile_pool(name="z0g", bufs=3))
         factor_pool = ctx.enter_context(tc.tile_pool(name="factor", bufs=2))
-        pair_pool = ctx.enter_context(tc.tile_pool(name="pair", bufs=3))
-        kron_pool = ctx.enter_context(tc.tile_pool(name="kron", bufs=2))
+        pair_pool = ctx.enter_context(tc.tile_pool(name="pair", bufs=2))
+        kron_pool = ctx.enter_context(tc.tile_pool(name="kron", bufs=3))
         group_pool = ctx.enter_context(tc.tile_pool(name="group", bufs=3))
         mx_pool = ctx.enter_context(tc.tile_pool(name="mx", bufs=3))
         res_pool = ctx.enter_context(tc.tile_pool(name="res", bufs=6))
         zt_psum = ctx.enter_context(tc.psum_pool(name="zt_psum", bufs=1))
-        turned_psum = ctx.enter_context(tc.psum_pool(name="turned_psum", bufs=3))
+        xt_psum = ctx.enter_context(tc.psum_pool(name="xt_psum", bufs=3))
         acc_psum = ctx.enter_context(tc.psum_pool(name="acc_psum", bufs=4))
 
         out_view = out.rearrange("(hq q) n -> q hq n", hq=2)
         zk_tiles = {}
-        z0g_tiles = {}
         zt_tiles = {}
         factor_tiles = {}
         pair_tiles = {}
@@ -59,159 +56,101 @@ def tile_fast_tucker_taylor_pa_t_kernel(tc, z, G2_words, G2_scales, out):
         def is_block(t):
             return 0 <= t < BLOCKS
 
-        def is_scalar_block(t):
-            return t % ROUND_BLOCKS >= VECTOR_BLOCKS
+        def starts_round(t):
+            return is_block(t) and t % ROUND_BLOCKS == 0
 
         def load_round(r):
-            samples = slice(ROUND * r, ROUND * (r + 1))
             zk = zk_pool.tile([P, 3, P], BF16, name="zk")
             zk_tiles[r] = zk
-            for j in (2, 1, 0):
+            for j in range(3):
                 nc.sync.dma_start(
                     out=zk[:, j, :],
-                    in_=z[j, :, samples].rearrange("r (ch m) -> r ch m", ch=ROUND_TILES),
+                    in_=z[j, :, ROUND * r : ROUND * (r + 1)].rearrange(
+                        "r (ch m) -> r ch m", ch=ROUND_TILES
+                    ),
                 )
-            width = VECTOR_BLOCKS * BLOCK
-            z0g = z0g_pool.tile([P, 4, width], BF16, name="z0g")
-            z0g_tiles[r] = z0g
-            piece = BLOCK if r == 0 else width
-            for first in range(0, width, piece):
-                for h in range(2):
-                    nc.sync.dma_start(
-                        out=z0g[h:P:2, :, first : first + piece],
-                        in_=z[0, 4 * h : 4 * h + 4, ROUND * r + first : ROUND * r + first + piece]
-                        .unsqueeze(0)
-                        .to_broadcast([P // 2, 4, piece]),
-                    )
 
         def turn_factors(r):
             zk = zk_tiles.pop(r)
             zt = zt_psum.tile([P, 3, P], BF16, name="zt")
             zt_tiles[r] = zt
-            for j in (2, 1, 0):
+            for j in range(3):
                 nc.tensor.transpose(zt[:, j, :], zk[:, j, :], ident_bf16[:])
 
         def copy_factors(r):
             zt = zt_tiles.pop(r)
-            z2T = factor_pool.tile([P, RANK, ROUND_TILES], F32, name="z2T")
-            z1T = factor_pool.tile([P, RANK, 2, ROUND_TILES], F32, name="z1T")
             z0T = factor_pool.tile([P, RANK, ROUND_TILES], F32, name="z0T")
-            factor_tiles[r] = (z0T, z1T, z2T)
-            nc.scalar.copy(out=z2T[:].rearrange("p c ch -> p (c ch)"), in_=zt[:, 2, :])
-            nc.scalar.copy(
-                out=z1T[:],
-                in_=zt[:, 1, :]
-                .rearrange("p (b ch) -> p b ch", b=RANK)
-                .unsqueeze(2)
-                .to_broadcast([P, RANK, 2, ROUND_TILES]),
-            )
+            z12T = factor_pool.tile([P, 2, RANK, ROUND_TILES], F32, name="z12T")
+            factor_tiles[r] = (z0T, z12T)
             nc.scalar.copy(
                 out=z0T[:].rearrange("p (u h e) ch -> p u h (e ch)", u=2, h=2),
                 in_=zt[:, 0, :].rearrange("p (h u x) -> p u h x", h=2, u=2),
             )
+            nc.scalar.copy(
+                out=z12T[:].rearrange("p j r ch -> p (j r ch)"),
+                in_=zt[:, 1:3, :].rearrange("p j x -> p (j x)"),
+            )
 
-        def pair_products(t):
-            z0T, z1T, z2T = factor_tiles[t // ROUND_BLOCKS]
-            tile0 = BLOCK_TILES * (t % ROUND_BLOCKS)
-            tiles = slice(tile0, tile0 + BLOCK_TILES)
-            if is_scalar_block(t):
-                w01 = pair_pool.tile([P, BLOCK_TILES, 2, RANK, 4], F32, name="w01")
-                pair_tiles[t] = w01
-                for u in range(2):
-                    nc.gpsimd.tensor_tensor(
-                        out=w01[:, :, u, :, :],
-                        in0=z0T[:, 4 * u : 4 * u + 4, tiles]
-                        .rearrange("p x i -> p i x")
-                        .unsqueeze(2)
-                        .to_broadcast([P, BLOCK_TILES, RANK, 4]),
-                        in1=z1T[:, :, 0, tiles]
-                        .rearrange("p b i -> p i b")
-                        .unsqueeze(3)
-                        .to_broadcast([P, BLOCK_TILES, RANK, 4]),
-                        op=MULT,
-                    )
-            else:
-                w12 = pair_pool.tile([P, BLOCK_TILES, RANK, 2 * RANK], F32, name="w12")
-                pair_tiles[t] = w12
-                nc.gpsimd.tensor_tensor(
-                    out=w12[:],
-                    in0=z2T[:, :, tiles]
-                    .rearrange("p c i -> p i c")
-                    .unsqueeze(3)
-                    .to_broadcast([P, BLOCK_TILES, RANK, 2 * RANK]),
-                    in1=z1T[:, :, :, tiles]
-                    .rearrange("p b h i -> p i (b h)")
+        def pair_products(r):
+            z0T, z12T = factor_tiles[r]
+            w01 = pair_pool.tile([P, ROUND_TILES, 2, RANK, 4], F32, name="w01")
+            pair_tiles[r] = w01
+            for u in range(2):
+                nc.vector.tensor_tensor(
+                    out=w01[:, :, u, :, :],
+                    in0=z0T[:, 4 * u : 4 * u + 4, :]
+                    .rearrange("p x i -> p i x")
                     .unsqueeze(2)
-                    .to_broadcast([P, BLOCK_TILES, RANK, 2 * RANK]),
+                    .to_broadcast([P, ROUND_TILES, RANK, 4]),
+                    in1=z12T[:, 0, :, :]
+                    .rearrange("p b i -> p i b")
+                    .unsqueeze(3)
+                    .to_broadcast([P, ROUND_TILES, RANK, 4]),
                     op=MULT,
                 )
 
-        def scalar_tile(t, ii):
-            z2T = factor_tiles[t // ROUND_BLOCKS][2]
-            if ii == 0:
-                kron_tiles[t] = kron_pool.tile([P, BLOCK_TILES, 2, RANK, 32], BF16, name="kronT")
-            kronT = kron_tiles[t]
-            tile_in_round = BLOCK_TILES * (t % ROUND_BLOCKS) + ii
-            pair = pair_tiles[t][:, ii].rearrange("p u b x -> p u (b x)")
-            for c in range(RANK):
-                nc.scalar.activation(
-                    out=kronT[:, ii, :, c, :],
-                    in_=pair,
-                    func=COPY,
-                    scale=z2T[:, c, tile_in_round : tile_in_round + 1],
-                )
+        def build(t):
+            r = t // ROUND_BLOCKS
+            z12T = factor_tiles[r][1]
+            w01 = pair_tiles[r]
+            kronT = kron_pool.tile([P, BLOCK_TILES, 2, RANK, 32], BF16, name="kronT")
+            kron_tiles[t] = kronT
+            for ii in range(BLOCK_TILES):
+                i = BLOCK_TILES * (t % ROUND_BLOCKS) + ii
+                pair = w01[:, i].rearrange("p u b x -> p u (b x)")
+                for c in range(RANK):
+                    z2 = z12T[:, 1, c, i : i + 1]
+                    if c < RANK - SCALAR_C:
+                        nc.vector.tensor_scalar(
+                            out=kronT[:, ii, :, c, :], in0=pair, scalar1=z2, scalar2=None, op0=MULT
+                        )
+                    else:
+                        nc.scalar.activation(out=kronT[:, ii, :, c, :], in_=pair, func=COPY, scale=z2)
 
         def turn(t):
+            kronT = kron_tiles.pop(t)
             turned_tiles[t] = []
-            if is_scalar_block(t):
-                kronT = kron_tiles.pop(t)
-                pair_tiles.pop(t)
-                for bank in range(2):
-                    xt = turned_psum.tile([P, 2, 2, P], F32, name="turned")
-                    turned_tiles[t].append(xt)
-                    for i2 in range(2):
-                        for u in range(2):
-                            nc.tensor.transpose(
-                                xt[:, i2, u, :],
-                                kronT[:, 2 * bank + i2, u].rearrange("p c x -> p (c x)").bitcast(F32),
-                                ident_f32[:],
-                            )
-            else:
-                w12 = pair_tiles.pop(t)
-                w12_k = turned_psum.tile([P, BLOCK_TILES, P], F32, name="turned")
-                turned_tiles[t].append(w12_k)
-                for ii in range(BLOCK_TILES):
-                    nc.tensor.transpose(
-                        w12_k[:, ii, :], w12[:, ii].rearrange("p c x -> p (c x)"), ident_f32[:]
-                    )
+            for bank in range(2):
+                xt = xt_psum.tile([P, 2, 2, P], F32, name="xt")
+                turned_tiles[t].append(xt)
+                for i2 in range(2):
+                    for u in range(2):
+                        nc.tensor.transpose(
+                            xt[:, i2, u, :],
+                            kronT[:, 2 * bank + i2, u].rearrange("p c x -> p (c x)").bitcast(F32),
+                            ident_f32[:],
+                        )
 
-        def group(t):
-            grouped = group_pool.tile([P, BLOCK, 4], BF16, align_bytes=64, name="grouped")
+        def regroup(t):
+            grouped = group_pool.tile([P, 4 * BLOCK], BF16, align_bytes=64, name="grouped")
             grouped_tiles[t] = grouped
-            turned = turned_tiles.pop(t)
-            if is_scalar_block(t):
-                grouped_words = (
-                    grouped[:]
-                    .rearrange("p n t -> p (n t)")
-                    .bitcast(F32)
-                    .rearrange("p (ii n u) -> p ii n u", ii=BLOCK_TILES, u=2)
-                )
-                for bank, xt in enumerate(turned):
-                    nc.scalar.copy(
-                        out=grouped_words[:, 2 * bank : 2 * bank + 2],
-                        in_=xt[:].rearrange("p s u n -> p s n u"),
-                    )
-            else:
-                first = BLOCK * (t % ROUND_BLOCKS)
-                z0g = z0g_tiles[t // ROUND_BLOCKS]
-                nc.vector.tensor_tensor(
-                    out=grouped[:],
-                    in0=z0g[:, :, first : first + BLOCK].rearrange("p t n -> p n t"),
-                    in1=turned[0][:]
-                    .rearrange("p i n -> p (i n)")
-                    .unsqueeze(2)
-                    .to_broadcast([P, BLOCK, 4]),
-                    op=MULT,
+            grouped_words = grouped[:].bitcast(F32).rearrange(
+                "p (ii n u) -> p ii n u", ii=BLOCK_TILES, u=2
+            )
+            for bank, xt in enumerate(turned_tiles.pop(t)):
+                nc.scalar.copy(
+                    out=grouped_words[:, 2 * bank : 2 * bank + 2],
+                    in_=xt[:].rearrange("p s u n -> p s n u"),
                 )
 
         def quantise(t):
@@ -219,11 +158,7 @@ def tile_fast_tucker_taylor_pa_t_kernel(tc, z, G2_words, G2_scales, out):
             codes = mx_pool.tile([P, BLOCK], U32, align_bytes=64, name="codes")
             scales = mx_pool.tile([P, BLOCK], U8, align_bytes=64, name="scales")
             mx_tiles[t] = (codes, scales)
-            nc.vector.quantize_mx(
-                out=codes[:].bitcast(FP8X4),
-                scales=scales[:],
-                in_=grouped[:].rearrange("p n t -> p (n t)"),
-            )
+            nc.vector.quantize_mx(out=codes[:].bitcast(FP8X4), scales=scales[:], in_=grouped[:])
 
         def multiply(t):
             codes, scales = mx_tiles.pop(t)
@@ -263,28 +198,24 @@ def tile_fast_tucker_taylor_pa_t_kernel(tc, z, G2_words, G2_scales, out):
                     in_=G2_scales[0, 4 * quad : 4 * quad + 4, :].bitcast(I32),
                 )
 
-            for step in range(-3, BLOCKS + 5):
-                if is_block(step - 2):
-                    group(step - 2)
+            for step in range(-3, BLOCKS + 4):
                 if is_block(step - 3):
                     quantise(step - 3)
-                if is_block(step + 3) and (step + 3) % ROUND_BLOCKS == 0:
+                if starts_round(step + 3):
                     turn_factors((step + 3) // ROUND_BLOCKS)
                 if is_block(step - 1):
                     turn(step - 1)
                 if is_block(step - 3):
                     multiply(step - 3)
-                if is_block(step + 2) and (step + 2) % ROUND_BLOCKS == 0:
+                if starts_round(step + 2):
                     copy_factors((step + 2) // ROUND_BLOCKS)
+                if is_block(step - 2):
+                    regroup(step - 2)
                 if is_block(step - 4):
                     store(step - 4)
+                if starts_round(step + 1):
+                    pair_products((step + 1) // ROUND_BLOCKS)
                 if is_block(step):
-                    in_round = step % ROUND_BLOCKS
-                    scalar_block = step - in_round + VECTOR_BLOCKS
-                    if not is_scalar_block(step):
-                        pair_products(step)
-                    if in_round == 0:
-                        pair_products(scalar_block)
-                    scalar_tile(scalar_block, in_round)
-                if is_block(step + 6) and (step + 6) % ROUND_BLOCKS == 0 and step + 6 > 0:
+                    build(step)
+                if starts_round(step + 6) and step + 6 > 0:
                     load_round((step + 6) // ROUND_BLOCKS)

@@ -22,7 +22,7 @@ BLOCKS = SAMPLES // BLOCK
 ROUND_BLOCKS = 4
 ROUND = ROUND_BLOCKS * BLOCK
 ROUND_TILES = ROUND // P
-SCALAR_C = 0
+HEAD_SCALAR_C = ()
 
 FLOPS = 2 * 256 * 512 * SAMPLES
 
@@ -109,22 +109,29 @@ def tile_fast_tucker_taylor_pa_t_kernel(tc, z, G2_words, G2_scales, out):
                     op=MULT,
                 )
 
-        def build(t):
+        def scalar_c(t, ii):
+            if t < len(HEAD_SCALAR_C):
+                return HEAD_SCALAR_C[t]
+            return 1 if ii >= BLOCK_TILES - 1 - t % 2 else 0
+
+        def build(t, on_scalar):
             r = t // ROUND_BLOCKS
             z12T = factor_tiles[r][1]
             w01 = pair_tiles[r]
-            kronT = kron_pool.tile([P, BLOCK_TILES, 2, RANK, 32], BF16, name="kronT")
-            kron_tiles[t] = kronT
+            if t not in kron_tiles:
+                kronT = kron_pool.tile([P, BLOCK_TILES, 2, RANK, 32], BF16, name="kronT")
+                kron_tiles[t] = kronT
+            kronT = kron_tiles[t]
             for ii in range(BLOCK_TILES):
                 i = BLOCK_TILES * (t % ROUND_BLOCKS) + ii
                 pair = w01[:, i].rearrange("p u b x -> p u (b x)")
                 for c in range(RANK):
                     z2 = z12T[:, 1, c, i : i + 1]
-                    if c < RANK - SCALAR_C:
+                    if c < RANK - scalar_c(t, ii) and not on_scalar:
                         nc.vector.tensor_scalar(
                             out=kronT[:, ii, :, c, :], in0=pair, scalar1=z2, scalar2=None, op0=MULT
                         )
-                    else:
+                    if c >= RANK - scalar_c(t, ii) and on_scalar:
                         nc.scalar.activation(out=kronT[:, ii, :, c, :], in_=pair, func=COPY, scale=z2)
 
         def turn(t):
@@ -184,6 +191,10 @@ def tile_fast_tucker_taylor_pa_t_kernel(tc, z, G2_words, G2_scales, out):
 
         with tc.manual_schedule():
             load_round(0)
+            warm_in = const.tile([P, 1], F32)
+            warm_out = const.tile([P, 1], F32)
+            nc.vector.memset(warm_in[:], 0.0)
+            nc.scalar.activation(out=warm_out[:], in_=warm_in[:], func=COPY)
             ident_bf16 = const.tile([P, P], BF16)
             make_identity(nc, ident_bf16[:])
             ident_f32 = const.tile([P, P], F32)
@@ -199,6 +210,8 @@ def tile_fast_tucker_taylor_pa_t_kernel(tc, z, G2_words, G2_scales, out):
                 )
 
             for step in range(-3, BLOCKS + 4):
+                if is_block(step):
+                    build(step, True)
                 if is_block(step - 3):
                     quantise(step - 3)
                 if starts_round(step + 3):
@@ -216,6 +229,6 @@ def tile_fast_tucker_taylor_pa_t_kernel(tc, z, G2_words, G2_scales, out):
                 if starts_round(step + 1):
                     pair_products((step + 1) // ROUND_BLOCKS)
                 if is_block(step):
-                    build(step)
+                    build(step, False)
                 if starts_round(step + 6) and step + 6 > 0:
                     load_round((step + 6) // ROUND_BLOCKS)

@@ -22,7 +22,8 @@ BLOCKS = SAMPLES // BLOCK
 ROUND_BLOCKS = 4
 ROUND = ROUND_BLOCKS * BLOCK
 ROUND_TILES = ROUND // P
-HEAD_SCALAR_C = ()
+HEAD_SCALAR_C = (3, 1)
+VECTOR_STORES_FROM = BLOCKS - 4
 
 FLOPS = 2 * 256 * 512 * SAMPLES
 
@@ -186,7 +187,10 @@ def tile_fast_tucker_taylor_pa_t_kernel(tc, z, G2_words, G2_scales, out):
         def store(t):
             for hq, acc in enumerate(acc_tiles.pop(t)):
                 res = res_pool.tile([P, BLOCK], F32, name="res")
-                nc.scalar.copy(out=res[:], in_=acc[:])
+                if hq == 1 and t >= VECTOR_STORES_FROM:
+                    nc.vector.tensor_copy(out=res[:], in_=acc[:])
+                else:
+                    nc.scalar.copy(out=res[:], in_=acc[:])
                 nc.sync.dma_start(out=out_view[:, hq, BLOCK * t : BLOCK * (t + 1)], in_=res[:])
 
         with tc.manual_schedule():

@@ -23,6 +23,7 @@ ROUND_BLOCKS = 4
 ROUND = ROUND_BLOCKS * BLOCK
 ROUND_TILES = ROUND // P
 HEAD_SCALAR_C = (3, 1)
+SCALAR_C_MAX = 3
 VECTOR_STORES_FROM = BLOCKS - 4
 
 FLOPS = 2 * 256 * 512 * SAMPLES
@@ -80,9 +81,10 @@ def tile_fast_tucker_taylor_pa_t_kernel(tc, z, G2_words, G2_scales, out):
 
         def copy_factors(r):
             zt = zt_tiles.pop(r)
-            z0T = factor_pool.tile([P, RANK, ROUND_TILES], F32, name="z0T")
-            z12T = factor_pool.tile([P, 2, RANK, ROUND_TILES], F32, name="z12T")
-            factor_tiles[r] = (z0T, z12T)
+            z0T = factor_pool.tile([P, RANK, ROUND_TILES], BF16, name="z0T")
+            z12T = factor_pool.tile([P, 2, RANK, ROUND_TILES], BF16, name="z12T")
+            z2S = factor_pool.tile([P, SCALAR_C_MAX, ROUND_TILES], F32, name="z2S")
+            factor_tiles[r] = (z0T, z12T, z2S)
             nc.scalar.copy(
                 out=z0T[:].rearrange("p (u h e) ch -> p u h (e ch)", u=2, h=2),
                 in_=zt[:, 0, :].rearrange("p (h u x) -> p u h x", h=2, u=2),
@@ -91,9 +93,13 @@ def tile_fast_tucker_taylor_pa_t_kernel(tc, z, G2_words, G2_scales, out):
                 out=z12T[:].rearrange("p j r ch -> p (j r ch)"),
                 in_=zt[:, 1:3, :].rearrange("p j x -> p (j x)"),
             )
+            nc.scalar.copy(
+                out=z2S[:].rearrange("p c ch -> p (c ch)"),
+                in_=zt[:, 2, (RANK - SCALAR_C_MAX) * ROUND_TILES :],
+            )
 
         def pair_products(r):
-            z0T, z12T = factor_tiles[r]
+            z0T, z12T = factor_tiles[r][0:2]
             w01 = pair_pool.tile([P, ROUND_TILES, 2, RANK, 4], F32, name="w01")
             pair_tiles[r] = w01
             for u in range(2):
@@ -113,11 +119,11 @@ def tile_fast_tucker_taylor_pa_t_kernel(tc, z, G2_words, G2_scales, out):
         def scalar_c(t, ii):
             if t < len(HEAD_SCALAR_C):
                 return HEAD_SCALAR_C[t]
-            return 1 if ii >= BLOCK_TILES - 1 - t % 2 else 0
+            return 1 if ii >= BLOCK_TILES - 1 - min(t % 4, 1) else 0
 
         def build(t, on_scalar):
             r = t // ROUND_BLOCKS
-            z12T = factor_tiles[r][1]
+            z12T, z2S = factor_tiles[r][1:3]
             w01 = pair_tiles[r]
             if t not in kron_tiles:
                 kronT = kron_pool.tile([P, BLOCK_TILES, 2, RANK, 32], BF16, name="kronT")
@@ -133,7 +139,12 @@ def tile_fast_tucker_taylor_pa_t_kernel(tc, z, G2_words, G2_scales, out):
                             out=kronT[:, ii, :, c, :], in0=pair, scalar1=z2, scalar2=None, op0=MULT
                         )
                     if c >= RANK - scalar_c(t, ii) and on_scalar:
-                        nc.scalar.activation(out=kronT[:, ii, :, c, :], in_=pair, func=COPY, scale=z2)
+                        nc.scalar.activation(
+                            out=kronT[:, ii, :, c, :],
+                            in_=pair,
+                            func=COPY,
+                            scale=z2S[:, c - (RANK - SCALAR_C_MAX), i : i + 1],
+                        )
 
         def turn(t):
             kronT = kron_tiles.pop(t)

@@ -16,15 +16,17 @@ COPY = mybir.ActivationFunctionType.Copy
 P = 128
 RANK = 8
 SAMPLES = 16384
-BLOCK = 512
-BLOCK_TILES = BLOCK // P
-BLOCKS = SAMPLES // BLOCK
-ROUND_BLOCKS = 4
-ROUND = ROUND_BLOCKS * BLOCK
-ROUND_TILES = ROUND // P
+TILES = SAMPLES // P
+ROUND_TILES = 16
+ROUND = ROUND_TILES * P
+FULL_BLOCK = 4
+TAIL_BLOCKS = (2, 1, 1)
+BLOCK_TILES = (FULL_BLOCK,) * ((TILES - sum(TAIL_BLOCKS)) // FULL_BLOCK) + TAIL_BLOCKS
+BLOCKS = len(BLOCK_TILES)
+FIRST_TILE = tuple(sum(BLOCK_TILES[:t]) for t in range(BLOCKS))
 HEAD_SCALAR_C = (3, 1)
 SCALAR_C_MAX = 3
-VECTOR_STORES_FROM = BLOCKS - 4
+VECTOR_STORES = 6
 
 FLOPS = 2 * 256 * 512 * SAMPLES
 
@@ -59,7 +61,17 @@ def tile_fast_tucker_taylor_pa_t_kernel(tc, z, G2_words, G2_scales, out):
             return 0 <= t < BLOCKS
 
         def starts_round(t):
-            return is_block(t) and t % ROUND_BLOCKS == 0
+            return is_block(t) and FIRST_TILE[t] % ROUND_TILES == 0
+
+        def round_of(t):
+            return FIRST_TILE[t] // ROUND_TILES
+
+        def scalar_c(t, ii):
+            if t < len(HEAD_SCALAR_C):
+                return HEAD_SCALAR_C[t]
+            if BLOCK_TILES[t] < FULL_BLOCK:
+                return 0
+            return 1 if ii >= FULL_BLOCK - 1 - min(t % 4, 1) else 0
 
         def load_round(r):
             zk = zk_pool.tile([P, 3, P], BF16, name="zk")
@@ -116,77 +128,79 @@ def tile_fast_tucker_taylor_pa_t_kernel(tc, z, G2_words, G2_scales, out):
                     op=MULT,
                 )
 
-        def scalar_c(t, ii):
-            if t < len(HEAD_SCALAR_C):
-                return HEAD_SCALAR_C[t]
-            return 1 if ii >= BLOCK_TILES - 1 - min(t % 4, 1) else 0
-
         def build(t, on_scalar):
-            r = t // ROUND_BLOCKS
-            z12T, z2S = factor_tiles[r][1:3]
-            w01 = pair_tiles[r]
+            z12T, z2S = factor_tiles[round_of(t)][1:3]
+            w01 = pair_tiles[round_of(t)]
             if t not in kron_tiles:
-                kronT = kron_pool.tile([P, BLOCK_TILES, 2, RANK, 32], BF16, name="kronT")
+                kronT = kron_pool.tile([P, BLOCK_TILES[t], 2, RANK, 32], BF16, name="kronT")
                 kron_tiles[t] = kronT
             kronT = kron_tiles[t]
-            for ii in range(BLOCK_TILES):
-                i = BLOCK_TILES * (t % ROUND_BLOCKS) + ii
+            for ii in range(BLOCK_TILES[t]):
+                i = FIRST_TILE[t] % ROUND_TILES + ii
                 pair = w01[:, i].rearrange("p u b x -> p u (b x)")
-                for c in range(RANK):
-                    z2 = z12T[:, 1, c, i : i + 1]
-                    if c < RANK - scalar_c(t, ii) and not on_scalar:
+                if on_scalar:
+                    for c in range(RANK - scalar_c(t, ii), RANK):
+                        z2 = z2S[:, c - (RANK - SCALAR_C_MAX), i : i + 1]
+                        nc.scalar.activation(out=kronT[:, ii, :, c, :], in_=pair, func=COPY, scale=z2)
+                else:
+                    for c in range(RANK - scalar_c(t, ii)):
+                        z2 = z12T[:, 1, c, i : i + 1]
                         nc.vector.tensor_scalar(
                             out=kronT[:, ii, :, c, :], in0=pair, scalar1=z2, scalar2=None, op0=MULT
-                        )
-                    if c >= RANK - scalar_c(t, ii) and on_scalar:
-                        nc.scalar.activation(
-                            out=kronT[:, ii, :, c, :],
-                            in_=pair,
-                            func=COPY,
-                            scale=z2S[:, c - (RANK - SCALAR_C_MAX), i : i + 1],
                         )
 
         def turn(t):
             kronT = kron_tiles.pop(t)
             turned_tiles[t] = []
-            for bank in range(2):
-                xt = xt_psum.tile([P, 2, 2, P], F32, name="xt")
-                turned_tiles[t].append(xt)
-                for i2 in range(2):
+            for first in range(0, BLOCK_TILES[t], 2):
+                count = min(2, BLOCK_TILES[t] - first)
+                xt = xt_psum.tile([P, count, 2, P], F32, name="xt")
+                turned_tiles[t].append((first, count, xt))
+                for i2 in range(count):
                     for u in range(2):
                         nc.tensor.transpose(
                             xt[:, i2, u, :],
-                            kronT[:, 2 * bank + i2, u].rearrange("p c x -> p (c x)").bitcast(F32),
+                            kronT[:, first + i2, u].rearrange("p c x -> p (c x)").bitcast(F32),
                             ident_f32[:],
                         )
 
+        def empty_bank(on_vector, out_ap, in_ap):
+            if on_vector:
+                nc.vector.tensor_copy(out=out_ap, in_=in_ap)
+            else:
+                nc.scalar.copy(out=out_ap, in_=in_ap)
+
         def regroup(t):
-            grouped = group_pool.tile([P, 4 * BLOCK], BF16, align_bytes=64, name="grouped")
+            grouped = group_pool.tile([P, 4 * P * BLOCK_TILES[t]], BF16, align_bytes=64, name="grouped")
             grouped_tiles[t] = grouped
             grouped_words = grouped[:].bitcast(F32).rearrange(
-                "p (ii n u) -> p ii n u", ii=BLOCK_TILES, u=2
+                "p (ii n u) -> p ii n u", ii=BLOCK_TILES[t], u=2
             )
-            for bank, xt in enumerate(turned_tiles.pop(t)):
-                nc.scalar.copy(
-                    out=grouped_words[:, 2 * bank : 2 * bank + 2],
-                    in_=xt[:].rearrange("p s u n -> p s n u"),
+            for first, count, xt in turned_tiles.pop(t):
+                empty_bank(
+                    False,
+                    grouped_words[:, first : first + count],
+                    xt[:].rearrange("p s u n -> p s n u"),
                 )
 
         def quantise(t):
             grouped = grouped_tiles.pop(t)
-            codes = mx_pool.tile([P, BLOCK], U32, align_bytes=64, name="codes")
-            scales = mx_pool.tile([P, BLOCK], U8, align_bytes=64, name="scales")
+            codes = mx_pool.tile([P, P * BLOCK_TILES[t]], U32, align_bytes=64, name="codes")
+            scales = mx_pool.tile([P, P * BLOCK_TILES[t]], U8, align_bytes=64, name="scales")
             mx_tiles[t] = (codes, scales)
             nc.vector.quantize_mx(out=codes[:].bitcast(FP8X4), scales=scales[:], in_=grouped[:])
 
         def multiply(t):
             codes, scales = mx_tiles.pop(t)
+            width = P * BLOCK_TILES[t]
+            halves_in_a_bank = 1 if BLOCK_TILES[t] == FULL_BLOCK else 2
             acc_tiles[t] = []
             for hq in range(2):
-                acc = acc_psum.tile([P, BLOCK], F32, name="acc")
-                acc_tiles[t].append(acc)
+                if hq % halves_in_a_bank == 0:
+                    acc = acc_psum.tile([P, halves_in_a_bank, width], F32, name="acc")
+                    acc_tiles[t].append(acc)
                 nc.tensor.matmul_mx(
-                    out=acc[:],
+                    out=acc[:, hq % halves_in_a_bank, :],
                     lhsT=g2_words[:, 256 * hq : 256 * (hq + 1)].bitcast(FP4X4),
                     lhsT_scale=g2_scales[:, P * hq : P * (hq + 1)],
                     rhs=codes[:].bitcast(FP8X4),
@@ -195,14 +209,22 @@ def tile_fast_tucker_taylor_pa_t_kernel(tc, z, G2_words, G2_scales, out):
                     stop=True,
                 )
 
-        def store(t):
-            for hq, acc in enumerate(acc_tiles.pop(t)):
-                res = res_pool.tile([P, BLOCK], F32, name="res")
-                if hq == 1 and t >= VECTOR_STORES_FROM:
-                    nc.vector.tensor_copy(out=res[:], in_=acc[:])
-                else:
-                    nc.scalar.copy(out=res[:], in_=acc[:])
-                nc.sync.dma_start(out=out_view[:, hq, BLOCK * t : BLOCK * (t + 1)], in_=res[:])
+        def store(t, bank, on_vector):
+            width = P * BLOCK_TILES[t]
+            acc = acc_tiles[t][bank]
+            halves = 2 // len(acc_tiles[t])
+            res = res_pool.tile([P, halves, width], F32, name="res")
+            empty_bank(on_vector, res[:], acc[:])
+            nc.sync.dma_start(
+                out=out_view[:, halves * bank : halves * (bank + 1), P * FIRST_TILE[t] : P * FIRST_TILE[t] + width],
+                in_=res[:],
+            )
+
+        def store_all(t):
+            banks = len(acc_tiles[t])
+            for bank in range(banks):
+                helps = t >= BLOCKS - VECTOR_STORES and (bank == 1 or (banks == 1 and t % 2 == 0))
+                store(t, bank, helps)
 
         with tc.manual_schedule():
             load_round(0)
@@ -230,20 +252,20 @@ def tile_fast_tucker_taylor_pa_t_kernel(tc, z, G2_words, G2_scales, out):
                 if is_block(step - 3):
                     quantise(step - 3)
                 if starts_round(step + 3):
-                    turn_factors((step + 3) // ROUND_BLOCKS)
+                    turn_factors(round_of(step + 3))
                 if is_block(step - 1):
                     turn(step - 1)
                 if is_block(step - 3):
                     multiply(step - 3)
                 if starts_round(step + 2):
-                    copy_factors((step + 2) // ROUND_BLOCKS)
+                    copy_factors(round_of(step + 2))
                 if is_block(step - 2):
                     regroup(step - 2)
                 if is_block(step - 4):
-                    store(step - 4)
+                    store_all(step - 4)
                 if starts_round(step + 1):
-                    pair_products((step + 1) // ROUND_BLOCKS)
+                    pair_products(round_of(step + 1))
                 if is_block(step):
                     build(step, False)
                 if starts_round(step + 6) and step + 6 > 0:
-                    load_round((step + 6) // ROUND_BLOCKS)
+                    load_round(round_of(step + 6))

@@ -24,7 +24,7 @@ TAIL_BLOCKS = (2, 1, 1)
 BLOCK_TILES = (FULL_BLOCK,) * ((TILES - sum(TAIL_BLOCKS)) // FULL_BLOCK) + TAIL_BLOCKS
 BLOCKS = len(BLOCK_TILES)
 FIRST_TILE = tuple(sum(BLOCK_TILES[:t]) for t in range(BLOCKS))
-HEAD_SCALAR_C = (3, 1)
+HEAD_SCALAR_C = (3, 1, 1, 1)
 SCALAR_C_MAX = 3
 VECTOR_STORES = 6
 

@@ -73,6 +73,11 @@ def tile_fast_tucker_taylor_pa_t_kernel(tc, z, G2_words, G2_scales, out):
                 return 0
             return 1 if ii >= FULL_BLOCK - 1 - min(t % 4, 1) else 0
 
+        def scalar_rows(r):
+            return max(
+                scalar_c(t, ii) for t in range(BLOCKS) if round_of(t) == r for ii in range(BLOCK_TILES[t])
+            )
+
         def load_round(r):
             zk = zk_pool.tile([P, 3, P], BF16, name="zk")
             zk_tiles[r] = zk
@@ -88,36 +93,34 @@ def tile_fast_tucker_taylor_pa_t_kernel(tc, z, G2_words, G2_scales, out):
             zk = zk_tiles.pop(r)
             zt = zt_psum.tile([P, 3, P], BF16, name="zt")
             zt_tiles[r] = zt
-            for j in range(3):
+            nc.tensor.transpose(zt[:, 0, :], zk[:, 0, :], reorder_bf16[:])
+            for j in range(1, 3):
                 nc.tensor.transpose(zt[:, j, :], zk[:, j, :], ident_bf16[:])
 
         def copy_factors(r):
             zt = zt_tiles.pop(r)
-            z0T = factor_pool.tile([P, RANK, ROUND_TILES], BF16, name="z0T")
             z12T = factor_pool.tile([P, 2, RANK, ROUND_TILES], BF16, name="z12T")
             z2S = factor_pool.tile([P, SCALAR_C_MAX, ROUND_TILES], F32, name="z2S")
-            factor_tiles[r] = (z0T, z12T, z2S)
-            nc.scalar.copy(
-                out=z0T[:].rearrange("p (u h e) ch -> p u h (e ch)", u=2, h=2),
-                in_=zt[:, 0, :].rearrange("p (h u x) -> p u h x", h=2, u=2),
-            )
+            factor_tiles[r] = (zt, z12T, z2S)
             nc.scalar.copy(
                 out=z12T[:].rearrange("p j r ch -> p (j r ch)"),
                 in_=zt[:, 1:3, :].rearrange("p j x -> p (j x)"),
             )
+            rows = scalar_rows(r)
             nc.scalar.copy(
-                out=z2S[:].rearrange("p c ch -> p (c ch)"),
-                in_=zt[:, 2, (RANK - SCALAR_C_MAX) * ROUND_TILES :],
+                out=z2S[:, SCALAR_C_MAX - rows :, :].rearrange("p c ch -> p (c ch)"),
+                in_=zt[:, 2, (RANK - rows) * ROUND_TILES :],
             )
 
         def pair_products(r):
-            z0T, z12T = factor_tiles[r][0:2]
+            zt, z12T = factor_tiles[r][0:2]
             w01 = pair_pool.tile([P, ROUND_TILES, 2, RANK, 4], F32, name="w01")
             pair_tiles[r] = w01
             for u in range(2):
                 nc.vector.tensor_tensor(
                     out=w01[:, :, u, :, :],
-                    in0=z0T[:, 4 * u : 4 * u + 4, :]
+                    in0=zt[:, 0, :]
+                    .rearrange("p (x i) -> p x i", i=ROUND_TILES)[:, 4 * u : 4 * u + 4, :]
                     .rearrange("p x i -> p i x")
                     .unsqueeze(2)
                     .to_broadcast([P, ROUND_TILES, RANK, 4]),
@@ -234,6 +237,11 @@ def tile_fast_tucker_taylor_pa_t_kernel(tc, z, G2_words, G2_scales, out):
             nc.scalar.activation(out=warm_out[:], in_=warm_in[:], func=COPY)
             ident_bf16 = const.tile([P, P], BF16)
             make_identity(nc, ident_bf16[:])
+            reorder_bf16 = const.tile([P, P], BF16)
+            nc.vector.tensor_copy(
+                out=reorder_bf16[:].rearrange("p (u h x) -> p u h x", u=2, h=2),
+                in_=ident_bf16[:].rearrange("p (h u x) -> p u h x", h=2, u=2),
+            )
             ident_f32 = const.tile([P, P], F32)
             make_identity(nc, ident_f32[:])
             g2_words = const.tile([P, 512], U8, align_bytes=64)

@@ -243,7 +243,7 @@ def tile_fast_tucker_taylor_pa_t_kernel(tc, z, G2_words, G2_scales, out):
                 in_=ident_bf16[:].rearrange("p (h u x) -> p u h x", h=2, u=2),
             )
             ident_f32 = const.tile([P, P], F32)
-            make_identity(nc, ident_f32[:])
+            nc.vector.tensor_copy(out=ident_f32[:], in_=ident_bf16[:])
             g2_words = const.tile([P, 512], U8, align_bytes=64)
             nc.sync.dma_start(out=g2_words[:].bitcast(I32), in_=G2_words[0].bitcast(I32))
             g2_scales = const.tile([P, 256], U8, align_bytes=64)

from contextlib import ExitStack

import concourse.mybir as mybir
from concourse.masks import make_identity

F32 = mybir.dt.float32
BF16 = mybir.dt.bfloat16
I32 = mybir.dt.int32
U32 = mybir.dt.uint32
U8 = mybir.dt.uint8
FP8X4 = mybir.dt.float8_e4m3fn_x4
FP4X4 = mybir.dt.float4_e2m1fn_x4
MULT = mybir.AluOpType.mult
COPY = mybir.ActivationFunctionType.Copy

P = 128
RANK = 8
SAMPLES = 16384
TILES = SAMPLES // P
ROUND_TILES = 16
ROUND = ROUND_TILES * P
FULL_BLOCK = 4
TAIL_BLOCKS = (2, 1, 1)
BLOCK_TILES = (FULL_BLOCK,) * ((TILES - sum(TAIL_BLOCKS)) // FULL_BLOCK) + TAIL_BLOCKS
BLOCKS = len(BLOCK_TILES)
FIRST_TILE = tuple(sum(BLOCK_TILES[:t]) for t in range(BLOCKS))
HEAD_SCALAR_C = (3, 1, 1, 1)
SCALAR_C_MAX = 3
VECTOR_STORES = 6

FLOPS = 2 * 256 * 512 * SAMPLES


def tile_fast_tucker_taylor_pa_t_kernel(tc, z, G2_words, G2_scales, out):
    nc = tc.nc
    with ExitStack() as ctx:
        const = ctx.enter_context(tc.tile_pool(name="const", bufs=1))
        zk_pool = ctx.enter_context(tc.tile_pool(name="zk", bufs=3))
        factor_pool = ctx.enter_context(tc.tile_pool(name="factor", bufs=2))
        pair_pool = ctx.enter_context(tc.tile_pool(name="pair", bufs=2))
        kron_pool = ctx.enter_context(tc.tile_pool(name="kron", bufs=3))
        group_pool = ctx.enter_context(tc.tile_pool(name="group", bufs=3))
        mx_pool = ctx.enter_context(tc.tile_pool(name="mx", bufs=3))
        res_pool = ctx.enter_context(tc.tile_pool(name="res", bufs=6))
        zt_psum = ctx.enter_context(tc.psum_pool(name="zt_psum", bufs=1))
        xt_psum = ctx.enter_context(tc.psum_pool(name="xt_psum", bufs=3))
        acc_psum = ctx.enter_context(tc.psum_pool(name="acc_psum", bufs=4))

        out_view = out.rearrange("(hq q) n -> q hq n", hq=2)
        zk_tiles = {}
        zt_tiles = {}
        factor_tiles = {}
        pair_tiles = {}
        kron_tiles = {}
        turned_tiles = {}
        grouped_tiles = {}
        mx_tiles = {}
        acc_tiles = {}

        def is_block(t):
            return 0 <= t < BLOCKS

        def starts_round(t):
            return is_block(t) and FIRST_TILE[t] % ROUND_TILES == 0

        def round_of(t):
            return FIRST_TILE[t] // ROUND_TILES

        def scalar_c(t, ii):
            if t < len(HEAD_SCALAR_C):
                return HEAD_SCALAR_C[t]
            if BLOCK_TILES[t] < FULL_BLOCK:
                return 0
            return 1 if ii >= FULL_BLOCK - 1 - min(t % 4, 1) else 0

        def scalar_rows(r):
            return max(
                scalar_c(t, ii) for t in range(BLOCKS) if round_of(t) == r for ii in range(BLOCK_TILES[t])
            )

        def load_round(r):
            zk = zk_pool.tile([P, 3, P], BF16, name="zk")
            zk_tiles[r] = zk
            for j in range(3):
                nc.sync.dma_start(
                    out=zk[:, j, :],
                    in_=z[j, :, ROUND * r : ROUND * (r + 1)].rearrange(
                        "r (ch m) -> r ch m", ch=ROUND_TILES
                    ),
                )

        def turn_factors(r):
            zk = zk_tiles.pop(r)
            zt = zt_psum.tile([P, 3, P], BF16, name="zt")
            zt_tiles[r] = zt
            nc.tensor.transpose(zt[:, 0, :], zk[:, 0, :], reorder_bf16[:])
            for j in range(1, 3):
                nc.tensor.transpose(zt[:, j, :], zk[:, j, :], ident_bf16[:])

        def copy_factors(r):
            zt = zt_tiles.pop(r)
            z12T = factor_pool.tile([P, 2, RANK, ROUND_TILES], BF16, name="z12T")
            z2S = factor_pool.tile([P, SCALAR_C_MAX, ROUND_TILES], F32, name="z2S")
            factor_tiles[r] = (zt, z12T, z2S)
            nc.scalar.copy(
                out=z12T[:].rearrange("p j r ch -> p (j r ch)"),
                in_=zt[:, 1:3, :].rearrange("p j x -> p (j x)"),
            )
            rows = scalar_rows(r)
            nc.scalar.copy(
                out=z2S[:, SCALAR_C_MAX - rows :, :].rearrange("p c ch -> p (c ch)"),
                in_=zt[:, 2, (RANK - rows) * ROUND_TILES :],
            )

        def pair_products(r):
            zt, z12T = factor_tiles[r][0:2]
            w01 = pair_pool.tile([P, ROUND_TILES, 2, RANK, 4], F32, name="w01")
            pair_tiles[r] = w01
            for u in range(2):
                nc.vector.tensor_tensor(
                    out=w01[:, :, u, :, :],
                    in0=zt[:, 0, :]
                    .rearrange("p (x i) -> p x i", i=ROUND_TILES)[:, 4 * u : 4 * u + 4, :]
                    .rearrange("p x i -> p i x")
                    .unsqueeze(2)
                    .to_broadcast([P, ROUND_TILES, RANK, 4]),
                    in1=z12T[:, 0, :, :]
                    .rearrange("p b i -> p i b")
                    .unsqueeze(3)
                    .to_broadcast([P, ROUND_TILES, RANK, 4]),
                    op=MULT,
                )

        def build(t, on_scalar):
            z12T, z2S = factor_tiles[round_of(t)][1:3]
            w01 = pair_tiles[round_of(t)]
            if t not in kron_tiles:
                kronT = kron_pool.tile([P, BLOCK_TILES[t], 2, RANK, 32], BF16, name="kronT")
                kron_tiles[t] = kronT
            kronT = kron_tiles[t]
            for ii in range(BLOCK_TILES[t]):
                i = FIRST_TILE[t] % ROUND_TILES + ii
                pair = w01[:, i].rearrange("p u b x -> p u (b x)")
                if on_scalar:
                    for c in range(RANK - scalar_c(t, ii), RANK):
                        z2 = z2S[:, c - (RANK - SCALAR_C_MAX), i : i + 1]
                        nc.scalar.activation(out=kronT[:, ii, :, c, :], in_=pair, func=COPY, scale=z2)
                else:
                    for c in range(RANK - scalar_c(t, ii)):
                        z2 = z12T[:, 1, c, i : i + 1]
                        nc.vector.tensor_scalar(
                            out=kronT[:, ii, :, c, :], in0=pair, scalar1=z2, scalar2=None, op0=MULT
                        )

        def turn(t):
            kronT = kron_tiles.pop(t)
            turned_tiles[t] = []
            for first in range(0, BLOCK_TILES[t], 2):
                count = min(2, BLOCK_TILES[t] - first)
                xt = xt_psum.tile([P, count, 2, P], F32, name="xt")
                turned_tiles[t].append((first, count, xt))
                for i2 in range(count):
                    for u in range(2):
                        nc.tensor.transpose(
                            xt[:, i2, u, :],
                            kronT[:, first + i2, u].rearrange("p c x -> p (c x)").bitcast(F32),
                            ident_f32[:],
                        )

        def empty_bank(on_vector, out_ap, in_ap):
            if on_vector:
                nc.vector.tensor_copy(out=out_ap, in_=in_ap)
            else:
                nc.scalar.copy(out=out_ap, in_=in_ap)

        def regroup(t):
            grouped = group_pool.tile([P, 4 * P * BLOCK_TILES[t]], BF16, align_bytes=64, name="grouped")
            grouped_tiles[t] = grouped
            grouped_words = grouped[:].bitcast(F32).rearrange(
                "p (ii n u) -> p ii n u", ii=BLOCK_TILES[t], u=2
            )
            for first, count, xt in turned_tiles.pop(t):
                empty_bank(
                    False,
                    grouped_words[:, first : first + count],
                    xt[:].rearrange("p s u n -> p s n u"),
                )

        def quantise(t):
            grouped = grouped_tiles.pop(t)
            codes = mx_pool.tile([P, P * BLOCK_TILES[t]], U32, align_bytes=64, name="codes")
            scales = mx_pool.tile([P, P * BLOCK_TILES[t]], U8, align_bytes=64, name="scales")
            mx_tiles[t] = (codes, scales)
            nc.vector.quantize_mx(out=codes[:].bitcast(FP8X4), scales=scales[:], in_=grouped[:])

        def multiply(t):
            codes, scales = mx_tiles.pop(t)
            width = P * BLOCK_TILES[t]
            halves_in_a_bank = 1 if BLOCK_TILES[t] == FULL_BLOCK else 2
            acc_tiles[t] = []
            for hq in range(2):
                if hq % halves_in_a_bank == 0:
                    acc = acc_psum.tile([P, halves_in_a_bank, width], F32, name="acc")
                    acc_tiles[t].append(acc)
                nc.tensor.matmul_mx(
                    out=acc[:, hq % halves_in_a_bank, :],
                    lhsT=g2_words[:, 256 * hq : 256 * (hq + 1)].bitcast(FP4X4),
                    lhsT_scale=g2_scales[:, P * hq : P * (hq + 1)],
                    rhs=codes[:].bitcast(FP8X4),
                    rhs_scale=scales[:],
                    start=True,
                    stop=True,
                )

        def store(t, bank, on_vector):
            width = P * BLOCK_TILES[t]
            acc = acc_tiles[t][bank]
            halves = 2 // len(acc_tiles[t])
            res = res_pool.tile([P, halves, width], F32, name="res")
            empty_bank(on_vector, res[:], acc[:])
            nc.sync.dma_start(
                out=out_view[:, halves * bank : halves * (bank + 1), P * FIRST_TILE[t] : P * FIRST_TILE[t] + width],
                in_=res[:],
            )

        def store_all(t):
            banks = len(acc_tiles[t])
            for bank in range(banks):
                helps = t >= BLOCKS - VECTOR_STORES and (bank == 1 or (banks == 1 and t % 2 == 0))
                store(t, bank, helps)

        with tc.manual_schedule():
            load_round(0)
            warm_in = const.tile([P, 1], F32)
            warm_out = const.tile([P, 1], F32)
            nc.vector.memset(warm_in[:], 0.0)
            nc.scalar.activation(out=warm_out[:], in_=warm_in[:], func=COPY)
            ident_bf16 = const.tile([P, P], BF16)
            make_identity(nc, ident_bf16[:])
            reorder_bf16 = const.tile([P, P], BF16)
            nc.vector.tensor_copy(
                out=reorder_bf16[:].rearrange("p (u h x) -> p u h x", u=2, h=2),
                in_=ident_bf16[:].rearrange("p (h u x) -> p u h x", h=2, u=2),
            )
            ident_f32 = const.tile([P, P], F32)
            nc.vector.tensor_copy(out=ident_f32[:], in_=ident_bf16[:])
            g2_words = const.tile([P, 512], U8, align_bytes=64)
            nc.sync.dma_start(out=g2_words[:].bitcast(I32), in_=G2_words[0].bitcast(I32))
            g2_scales = const.tile([P, 256], U8, align_bytes=64)
            nc.vector.memset(g2_scales[:].bitcast(I32), 0)
            for quad in range(4):
                nc.sync.dma_start(
                    out=g2_scales[32 * quad : 32 * quad + 4, :].bitcast(I32),
                    in_=G2_scales[0, 4 * quad : 4 * quad + 4, :].bitcast(I32),
                )

            for step in range(-3, BLOCKS + 4):
                if is_block(step):
                    build(step, True)
                if is_block(step - 3):
                    quantise(step - 3)
                if starts_round(step + 3):
                    turn_factors(round_of(step + 3))
                if is_block(step - 1):
                    turn(step - 1)
                if is_block(step - 3):
                    multiply(step - 3)
                if starts_round(step + 2):
                    copy_factors(round_of(step + 2))
                if is_block(step - 2):
                    regroup(step - 2)
                if is_block(step - 4):
                    store_all(step - 4)
                if starts_round(step + 1):
                    pair_products(round_of(step + 1))
                if is_block(step):
                    build(step, False)
                if starts_round(step + 6) and step + 6 > 0:
                    load_round(round_of(step + 6))
